import numpy as np
import ml_dtypes


def mxq(x, axis, fmt="e4m3"):
    dtype, down = {"e4m3": (ml_dtypes.float8_e4m3fn, 7), "e5m2": (ml_dtypes.float8_e5m2, 14)}[fmt]
    v = np.moveaxis(np.asarray(x, np.float32).astype(ml_dtypes.bfloat16).astype(np.float64), axis, -1)
    blocks = v.reshape(v.shape[:-1] + (-1, 32))
    amax = np.abs(blocks).max(-1, keepdims=True)
    byte = np.maximum(np.where(amax > 0, np.frexp(amax)[1] - 1 + 127, 0) - down, 1)
    scale = np.exp2(byte - 127.0)
    codes = (blocks / scale).astype(np.float32).astype(dtype).astype(np.float64)
    return np.moveaxis((codes * scale).reshape(v.shape), -1, axis)


WIDE = False


def mx_kscale(k):
    if not WIDE:
        return np.ones(k)
    levels = np.array([10, -10, 5, -5, 0])
    a = np.random.permutation(np.resize(levels, k // 512 * 4)).reshape(k // 512, 4)
    idx = np.arange(k)
    return np.exp2(a[idx // 512, idx % 128 // 32])


BF16 = ml_dtypes.bfloat16


def bf(x):
    return np.asarray(x, np.float32).astype(BF16)


def f64(x):
    return np.asarray(x).astype(np.float64)


E2M1 = np.array([0.0, 0.5, 1.0, 1.5, 2.0, 3.0, 4.0, 6.0, -0.0, -0.5, -1.0, -1.5, -2.0, -3.0, -4.0, -6.0])


def pack_weight(w, fmt):
    k, n = w.shape
    w = f64(bf(w)).reshape(k // 32, 32, n)
    amax = np.abs(w).max(1)
    if fmt == "e4m3":
        byte = np.frexp(amax)[1] - 1 + 127 - 7
    else:
        mant, ex = np.frexp(amax / 6.0)
        byte = np.where(mant > 0.5, ex, ex - 1) + 127
    byte = np.clip(np.where(amax > 0, byte, 1), 1, 254)
    scaled = (w * np.exp2(127.0 - byte)[:, None, :]).reshape(k, n).astype(np.float32)
    by_word = np.ascontiguousarray(scaled.reshape(k // 512, 128, 4, n).transpose(0, 1, 3, 2))
    if fmt == "e4m3":
        words = by_word.astype(ml_dtypes.float8_e4m3fn).view(np.uint8)
    else:
        c = by_word.astype(ml_dtypes.float4_e2m1fn).view(np.uint8) & 0xF
        words = c[..., 0::2] | (c[..., 1::2] << 4)
    return np.ascontiguousarray(words), np.ascontiguousarray(byte.astype(np.uint8).reshape(k // 512, 16, n))


def unpack_weight(words, scales, fmt):
    g, p, n, _ = words.shape
    if fmt == "e4m3":
        vals = np.ascontiguousarray(words).view(ml_dtypes.float8_e4m3fn).astype(np.float64)
    else:
        nib = np.empty((g, p, n, 4), np.uint8)
        nib[..., 0::2] = words & 0xF
        nib[..., 1::2] = words >> 4
        vals = E2M1[nib]
    vals = vals * np.repeat(np.exp2(scales.astype(np.float64) - 127.0), 8, axis=1)[..., None]
    return vals.transpose(0, 1, 3, 2).reshape(g * 512, n)

def pack4(w):
    words, scales = pack_weight(w, "e2m1")
    return words.reshape(words.shape[0], 128, -1), scales


def unpack4(words, scales):
    return unpack_weight(words.reshape(words.shape[0], 128, -1, 2), scales, "e2m1")


B, C, H, W = 4, 512, 64, 32
CH = C // 2
N = H * W
QS = 1.35 * CH ** -0.25


def pool2(t):
    r = t.reshape(B, -1, H // 2, 2, W // 2, 2)
    return r.max(axis=(3, 5)) + r.mean(axis=(3, 5))


def setup_inputs():
    s = mx_kscale(C)
    x = bf(np.random.standard_normal((B, C, H, W)) * s[None, :, None, None])
    w1 = np.random.standard_normal((CH, C)) * QS / np.sqrt(C) / s
    w2 = np.random.standard_normal((CH, C)) * QS / np.sqrt(C) / s
    W1_words, W1_scales = pack4(np.ascontiguousarray(w1.T))
    W2_words, W2_scales = pack4(np.ascontiguousarray(w2.T))
    return {"x": x,
            "W1_words": W1_words, "W1_scales": W1_scales,
            "W2_words": W2_words, "W2_scales": W2_scales}


def reference(x, W1_words, W1_scales, W2_words, W2_scales):
    xq = mxq(f64(x).reshape(B, C, N), 1, "e4m3")
    c1 = unpack4(W1_words, W1_scales).T @ xq
    c2 = unpack4(W2_words, W2_scales).T @ xq
    return pool2(c1.reshape(B, CH, H, W)), c2.reshape(B, CH, H, W)

@@ -1,0 +1,185 @@
+from contextlib import ExitStack
+
+import concourse.mybir as mybir
+
+BF16 = mybir.dt.bfloat16
+F32 = mybir.dt.float32
+I32 = mybir.dt.int32
+U8 = mybir.dt.uint8
+U32 = mybir.dt.uint32
+FP8X4 = mybir.dt.float8_e4m3fn_x4
+FP4X4 = mybir.dt.float4_e2m1fn_x4
+
+P = 128
+PACK = 4
+IMAGES, CHANNELS, HEIGHT, WIDTH = 4, 512, 64, 32
+PIXELS = HEIGHT * WIDTH
+OUT_CHANNELS = 256
+HALVES = OUT_CHANNELS // P
+
+CHUNK = 512
+CHUNK_ROWS = CHUNK // WIDTH
+CHUNKS_PER_IMAGE = PIXELS // CHUNK
+CHUNKS = IMAGES * CHUNKS_PER_IMAGE
+WINDOW = 4
+POOLED = CHUNK // WINDOW
+PAIR = 2
+
+FLOPS = 2 * IMAGES * PIXELS * CHANNELS * 2 * OUT_CHANNELS
+
+
+def tile_selfspatialattentionmodule_pa_t_kernel(
+    tc, x, W1_words, W1_scales, W2_words, W2_scales, out_0, out_1
+):
+    nc = tc.nc
+    assert tuple(x.shape) == (IMAGES, CHANNELS, HEIGHT, WIDTH)
+
+    x_rows = x.rearrange("b (p t) r w -> b p t (r w)", t=PACK)
+    pooled_rows = out_0.rearrange("b (half p) r w -> b p half (r w)", p=P)
+    conv2_rows = out_1.rearrange("b (half p) r w -> b p half (r w)", p=P)
+
+    with ExitStack() as ctx:
+        keep = ctx.enter_context(tc.tile_pool(name="keep", bufs=1))
+        grouped_pool = ctx.enter_context(tc.tile_pool(name="grouped", bufs=3))
+        packed_pool = ctx.enter_context(tc.tile_pool(name="packed", bufs=3))
+        conv2_pool = ctx.enter_context(tc.tile_pool(name="conv2", bufs=3))
+        pooled_pool = ctx.enter_context(tc.tile_pool(name="pooled", bufs=2))
+        conv1_banks = ctx.enter_context(tc.psum_pool(name="conv1_banks", bufs=3))
+        conv2_banks = ctx.enter_context(tc.psum_pool(name="conv2_banks", bufs=3))
+        sum_banks = ctx.enter_context(tc.psum_pool(name="sum_banks", bufs=2))
+        ctx.enter_context(tc.manual_schedule())
+
+        raw = [keep.tile([P, PACK, PIXELS], BF16, name="raw%d" % b) for b in range(IMAGES)]
+        w_words = keep.tile([P, 2, 2 * OUT_CHANNELS], U8, align_bytes=64)
+        w_scales = keep.tile([P, 2, OUT_CHANNELS], U8, align_bytes=64)
+
+        def load_x(b, first_chunk, chunks):
+            cols = slice(first_chunk * CHUNK, (first_chunk + chunks) * CHUNK)
+            nc.sync.dma_start(out=raw[b][:, :, cols], in_=x_rows[b][:, :, cols])
+
+        def load_weight(w, words, scales):
+            nc.sync.dma_start(out=w_words[:, w, :].bitcast(I32), in_=words[0].bitcast(I32))
+            for quadrant in range(4):
+                nc.sync.dma_start(
+                    out=w_scales[32 * quadrant : 32 * (quadrant + 1), w, :].bitcast(I32),
+                    in_=scales[0, 4 * quadrant : 4 * (quadrant + 1), :]
+                    .bitcast(I32)
+                    .unsqueeze(0)
+                    .broadcast_to([8, 4, OUT_CHANNELS // 4]),
+                )
+
+        load_x(0, 0, 1)
+        load_weight(0, W1_words, W1_scales)
+        load_x(0, 1, 1)
+        load_x(0, 2, 2)
+        load_weight(1, W2_words, W2_scales)
+        for b in range(1, IMAGES):
+            load_x(b, 0, CHUNKS_PER_IMAGE)
+
+        grouped = {}
+        codes = {}
+        scales_of = {}
+        conv1 = {}
+        conv2 = {}
+        sums = {}
+        maxima = {}
+        conv2_out = {}
+        pooled_out = {}
+
+        def regroup(c):
+            b, k = divmod(c, CHUNKS_PER_IMAGE)
+            grouped[c] = grouped_pool.tile([P, PACK * CHUNK], BF16, name="grouped", align_bytes=64)
+            src = raw[b][:, :, k * CHUNK : (k + 1) * CHUNK].rearrange(
+                "p t (i dh jq jr dw) -> p dh i jq t jr dw", i=CHUNK_ROWS // 2, dh=2, jq=WIDTH // 4, jr=2, dw=2
+            )
+            dst = grouped[c][:].rearrange(
+                "p (dh dw i jq jr t) -> p dh i jq t jr dw", dh=2, dw=2, i=CHUNK_ROWS // 2, jq=WIDTH // 4, jr=2, t=PACK
+            )
+            nc.scalar.copy(out=dst[:, 0], in_=src[:, 0])
+            nc.vector.tensor_copy(out=dst[:, 1], in_=src[:, 1])
+
+        def quantise(c):
+            codes[c] = packed_pool.tile([P, CHUNK], U32, name="codes", align_bytes=64)
+            scales_of[c] = packed_pool.tile([P, CHUNK], U8, name="scales", align_bytes=64)
+            nc.vector.quantize_mx(out=codes[c][:].bitcast(FP8X4), scales=scales_of[c][:], in_=grouped[c][:])
+
+        def multiply_by(w, half, out, c, cols, start, stop):
+            nc.tensor.matmul_mx(
+                out=out,
+                lhsT=w_words[:, w, half * 2 * P : (half + 1) * 2 * P].bitcast(FP4X4),
+                lhsT_scale=w_scales[:, w, half * P : (half + 1) * P],
+                rhs=codes[c][:, cols].bitcast(FP8X4),
+                rhs_scale=scales_of[c][:, cols],
+                start=start,
+                stop=stop,
+            )
+
+        def multiply(c):
+            pair, k = divmod(c, PAIR)
+            for half in range(HALVES):
+                conv1[c, half] = conv1_banks.tile([P, CHUNK], F32, name="conv1")
+                multiply_by(0, half, conv1[c, half][:], c, slice(0, CHUNK), True, True)
+            for half in range(HALVES):
+                conv2[c, half] = conv2_banks.tile([P, CHUNK], F32, name="conv2")
+                multiply_by(1, half, conv2[c, half][:], c, slice(0, CHUNK), True, True)
+            if k == 0:
+                sums[pair] = sum_banks.tile([P, HALVES * PAIR * POOLED], F32, name="sums")
+            for half in range(HALVES):
+                group = slice((half * PAIR + k) * POOLED, (half * PAIR + k + 1) * POOLED)
+                for place in range(WINDOW):
+                    multiply_by(
+                        0,
+                        half,
+                        sums[pair][:, group],
+                        c,
+                        slice(place * POOLED, (place + 1) * POOLED),
+                        place == 0,
+                        place == WINDOW - 1,
+                    )
+
+        def drain(c):
+            pair, k = divmod(c, PAIR)
+            b, pair_of_image = divmod(pair, CHUNKS_PER_IMAGE // PAIR)
+            if k == 0:
+                conv2_out[pair] = conv2_pool.tile([P, HALVES, PAIR * CHUNK], F32, name="conv2_out")
+                maxima[pair] = pooled_pool.tile([P, HALVES * PAIR * POOLED], F32, name="maxima")
+            if c % CHUNKS_PER_IMAGE == 0:
+                pooled_out[b] = pooled_pool.tile([P, HALVES, PIXELS // WINDOW], F32, name="pooled_out")
+            for half in range(HALVES):
+                nc.scalar.copy(
+                    out=conv2_out[pair][:, half, k * CHUNK : (k + 1) * CHUNK].rearrange(
+                        "p (i dh j dw) -> p dh i j dw", i=CHUNK_ROWS // 2, dh=2, j=WIDTH // 2, dw=2
+                    ),
+                    in_=conv2[c, half][:].rearrange("p (dh dw i j) -> p dh i j dw", dh=2, dw=2, i=CHUNK_ROWS // 2, j=WIDTH // 2
+                    ),
+                )
+                nc.vector.tensor_reduce(
+                    out=maxima[pair][:, (half * PAIR + k) * POOLED : (half * PAIR + k + 1) * POOLED],
+                    in_=conv1[c, half][:].rearrange("p (place m) -> p m place", place=WINDOW),
+                    axis=mybir.AxisListType.X,
+                    op=mybir.AluOpType.max,
+                )
+            if k == PAIR - 1:
+                nc.sync.dma_start(
+                    out=conv2_rows[b][:, :, pair_of_image * PAIR * CHUNK : (pair_of_image + 1) * PAIR * CHUNK],
+                    in_=conv2_out[pair][:],
+                )
+                nc.vector.scalar_tensor_tensor(
+                    out=pooled_out[b][:, :, pair_of_image * PAIR * POOLED : (pair_of_image + 1) * PAIR * POOLED],
+                    in0=sums[pair][:].rearrange("p (half m) -> p half m", half=HALVES),
+                    scalar=1.0 / WINDOW,
+                    in1=maxima[pair][:].rearrange("p (half m) -> p half m", half=HALVES),
+                    op0=mybir.AluOpType.mult,
+                    op1=mybir.AluOpType.add,
+                )
+            if c % CHUNKS_PER_IMAGE == CHUNKS_PER_IMAGE - 1:
+                nc.sync.dma_start(out=pooled_rows[b], in_=pooled_out[b][:])
+
+        for step in range(CHUNKS + 2):
+            if step < CHUNKS:
+                regroup(step)
+            if 1 <= step <= CHUNKS:
+                quantise(step - 1)
+                multiply(step - 1)
+            if step >= 2:
+                drain(step - 2)

@@ -49,13 +49,16 @@ def tile_selfspatialattentionmodule_pa_t_kernel(
         sum_banks = ctx.enter_context(tc.psum_pool(name="sum_banks", bufs=2))
         ctx.enter_context(tc.manual_schedule())
 
-        raw = [keep.tile([P, PACK, PIXELS], BF16, name="raw%d" % b) for b in range(IMAGES)]
+        raw = {}
         w_words = keep.tile([P, 2, 2 * OUT_CHANNELS], U8, align_bytes=64)
         w_scales = keep.tile([P, 2, OUT_CHANNELS], U8, align_bytes=64)
 
-        def load_x(b, first_chunk, chunks):
-            cols = slice(first_chunk * CHUNK, (first_chunk + chunks) * CHUNK)
-            nc.sync.dma_start(out=raw[b][:, :, cols], in_=x_rows[b][:, :, cols])
+        def load_x(first_chunk, chunks):
+            b, k = divmod(first_chunk, CHUNKS_PER_IMAGE)
+            piece = keep.tile([P, PACK, chunks * CHUNK], BF16, name="raw%d" % first_chunk)
+            nc.sync.dma_start(out=piece[:], in_=x_rows[b][:, :, k * CHUNK : (k + chunks) * CHUNK])
+            for n in range(chunks):
+                raw[first_chunk + n] = piece[:, :, n * CHUNK : (n + 1) * CHUNK]
 
         def load_weight(w, words, scales):
             nc.sync.dma_start(out=w_words[:, w, :].bitcast(I32), in_=words[0].bitcast(I32))
@@ -68,13 +71,13 @@ def tile_selfspatialattentionmodule_pa_t_kernel(
                     .broadcast_to([8, 4, OUT_CHANNELS // 4]),
                 )
 
-        load_x(0, 0, 1)
+        load_x(0, 1)
         load_weight(0, W1_words, W1_scales)
-        load_x(0, 1, 1)
-        load_x(0, 2, 2)
+        load_x(1, 1)
+        load_x(2, 2)
         load_weight(1, W2_words, W2_scales)
         for b in range(1, IMAGES):
-            load_x(b, 0, CHUNKS_PER_IMAGE)
+            load_x(b * CHUNKS_PER_IMAGE, CHUNKS_PER_IMAGE)
 
         grouped = {}
         codes = {}
@@ -87,9 +90,8 @@ def tile_selfspatialattentionmodule_pa_t_kernel(
         pooled_out = {}
 
         def regroup(c):
-            b, k = divmod(c, CHUNKS_PER_IMAGE)
             grouped[c] = grouped_pool.tile([P, PACK * CHUNK], BF16, name="grouped", align_bytes=64)
-            src = raw[b][:, :, k * CHUNK : (k + 1) * CHUNK].rearrange(
+            src = raw[c].rearrange(
                 "p t (i dh jq jr dw) -> p dh i jq t jr dw", i=CHUNK_ROWS // 2, dh=2, jq=WIDTH // 4, jr=2, dw=2
             )
             dst = grouped[c][:].rearrange(
@@ -159,11 +161,17 @@ def tile_selfspatialattentionmodule_pa_t_kernel(
                     axis=mybir.AxisListType.X,
                     op=mybir.AluOpType.max,
                 )
-            if k == PAIR - 1:
+            if pair == CHUNKS // PAIR - 1:
+                nc.sync.dma_start(
+                    out=conv2_rows[b][:, :, (c % CHUNKS_PER_IMAGE) * CHUNK : (c % CHUNKS_PER_IMAGE + 1) * CHUNK],
+                    in_=conv2_out[pair][:, :, k * CHUNK : (k + 1) * CHUNK],
+                )
+            elif k == PAIR - 1:
                 nc.sync.dma_start(
                     out=conv2_rows[b][:, :, pair_of_image * PAIR * CHUNK : (pair_of_image + 1) * PAIR * CHUNK],
                     in_=conv2_out[pair][:],
                 )
+            if k == PAIR - 1:
                 nc.vector.scalar_tensor_tensor(
                     out=pooled_out[b][:, :, pair_of_image * PAIR * POOLED : (pair_of_image + 1) * PAIR * POOLED],
                     in0=sums[pair][:].rearrange("p (half m) -> p half m", half=HALVES),
@@ -172,7 +180,10 @@ def tile_selfspatialattentionmodule_pa_t_kernel(
                     op0=mybir.AluOpType.mult,
                     op1=mybir.AluOpType.add,
                 )
-            if c % CHUNKS_PER_IMAGE == CHUNKS_PER_IMAGE - 1:
+            if b == IMAGES - 1 and k == PAIR - 1:
+                cols = slice(pair_of_image * PAIR * POOLED, (pair_of_image + 1) * PAIR * POOLED)
+                nc.sync.dma_start(out=pooled_rows[b][:, :, cols], in_=pooled_out[b][:, :, cols])
+            elif c % CHUNKS_PER_IMAGE == CHUNKS_PER_IMAGE - 1:
                 nc.sync.dma_start(out=pooled_rows[b], in_=pooled_out[b][:])
 
         for step in range(CHUNKS + 2):

@@ -91,14 +91,24 @@ def tile_selfspatialattentionmodule_pa_t_kernel(
 
         def regroup(c):
             grouped[c] = grouped_pool.tile([P, PACK * CHUNK], BF16, name="grouped", align_bytes=64)
-            src = raw[c].rearrange(
-                "p t (i dh jq jr dw) -> p dh i jq t jr dw", i=CHUNK_ROWS // 2, dh=2, jq=WIDTH // 4, jr=2, dw=2
+            nc.scalar.copy(
+                out=grouped[c][:].rearrange(
+                    "p (dh dw i jq jr t) -> p dh i jq t jr dw", dh=2, dw=2, i=CHUNK_ROWS // 2, jq=WIDTH // 4, jr=2, t=PACK
+                )[:, 0],
+                in_=raw[c].rearrange(
+                    "p t (i dh jq jr dw) -> p dh i jq t jr dw", i=CHUNK_ROWS // 2, dh=2, jq=WIDTH // 4, jr=2, dw=2
+                )[:, 0],
             )
-            dst = grouped[c][:].rearrange(
-                "p (dh dw i jq jr t) -> p dh i jq t jr dw", dh=2, dw=2, i=CHUNK_ROWS // 2, jq=WIDTH // 4, jr=2, t=PACK
+            nc.gpsimd.tensor_scalar(
+                out=grouped[c][:].rearrange(
+                    "p (dh dw i j t) -> p dh i j dw t", dh=2, dw=2, i=CHUNK_ROWS // 2, j=WIDTH // 2, t=PACK
+                )[:, 1],
+                in0=raw[c].rearrange("p t (i dh j dw) -> p dh i j dw t", i=CHUNK_ROWS // 2, dh=2, j=WIDTH // 2, dw=2)[:, 1],
+                scalar1=1.0,
+                scalar2=0.0,
+                op0=mybir.AluOpType.mult,
+                op1=mybir.AluOpType.add,
             )
-            nc.scalar.copy(out=dst[:, 0], in_=src[:, 0])
-            nc.vector.tensor_copy(out=dst[:, 1], in_=src[:, 1])
 
         def quantise(c):
             codes[c] = packed_pool.tile([P, CHUNK], U32, name="codes", align_bytes=64)

@@ -24,6 +24,7 @@ CHUNKS = IMAGES * CHUNKS_PER_IMAGE
 WINDOW = 4
 POOLED = CHUNK // WINDOW
 PAIR = 2
+PAIRS_PER_IMAGE = CHUNKS_PER_IMAGE // PAIR
 
 FLOPS = 2 * IMAGES * PIXELS * CHANNELS * 2 * OUT_CHANNELS
 
@@ -150,19 +151,23 @@ def tile_selfspatialattentionmodule_pa_t_kernel(
                     )
 
         def drain(c):
+            b = c // CHUNKS_PER_IMAGE
             pair, k = divmod(c, PAIR)
-            b, pair_of_image = divmod(pair, CHUNKS_PER_IMAGE // PAIR)
+            chunks_stored = 1 if pair == CHUNKS // PAIR - 1 else PAIR
+            pairs_stored = 1 if b == IMAGES - 1 else PAIRS_PER_IMAGE
+            first_chunk = c - c % chunks_stored
+            first_pair = pair - pair % pairs_stored
+            if c == first_chunk:
+                conv2_out[first_chunk] = conv2_pool.tile([P, HALVES, chunks_stored * CHUNK], F32, name="conv2_out")
             if k == 0:
-                conv2_out[pair] = conv2_pool.tile([P, HALVES, PAIR * CHUNK], F32, name="conv2_out")
                 maxima[pair] = pooled_pool.tile([P, HALVES * PAIR * POOLED], F32, name="maxima")
-            if c % CHUNKS_PER_IMAGE == 0:
-                pooled_out[b] = pooled_pool.tile([P, HALVES, PIXELS // WINDOW], F32, name="pooled_out")
             for half in range(HALVES):
                 nc.scalar.copy(
-                    out=conv2_out[pair][:, half, k * CHUNK : (k + 1) * CHUNK].rearrange(
+                    out=conv2_out[first_chunk][:, half, (c - first_chunk) * CHUNK : (c - first_chunk + 1) * CHUNK].rearrange(
                         "p (i dh j dw) -> p dh i j dw", i=CHUNK_ROWS // 2, dh=2, j=WIDTH // 2, dw=2
                     ),
-                    in_=conv2[c, half][:].rearrange("p (dh dw i j) -> p dh i j dw", dh=2, dw=2, i=CHUNK_ROWS // 2, j=WIDTH // 2
+                    in_=conv2[c, half][:].rearrange(
+                        "p (dh dw i j) -> p dh i j dw", dh=2, dw=2, i=CHUNK_ROWS // 2, j=WIDTH // 2
                     ),
                 )
                 nc.vector.tensor_reduce(
@@ -171,30 +176,32 @@ def tile_selfspatialattentionmodule_pa_t_kernel(
                     axis=mybir.AxisListType.X,
                     op=mybir.AluOpType.max,
                 )
-            if pair == CHUNKS // PAIR - 1:
+            if c == first_chunk + chunks_stored - 1:
+                start = (first_chunk % CHUNKS_PER_IMAGE) * CHUNK
                 nc.sync.dma_start(
-                    out=conv2_rows[b][:, :, (c % CHUNKS_PER_IMAGE) * CHUNK : (c % CHUNKS_PER_IMAGE + 1) * CHUNK],
-                    in_=conv2_out[pair][:, :, k * CHUNK : (k + 1) * CHUNK],
-                )
-            elif k == PAIR - 1:
-                nc.sync.dma_start(
-                    out=conv2_rows[b][:, :, pair_of_image * PAIR * CHUNK : (pair_of_image + 1) * PAIR * CHUNK],
-                    in_=conv2_out[pair][:],
+                    out=conv2_rows[b][:, :, start : start + chunks_stored * CHUNK], in_=conv2_out[first_chunk][:]
                 )
             if k == PAIR - 1:
+                if pair == first_pair:
+                    pooled_out[first_pair] = pooled_pool.tile(
+                        [P, HALVES, pairs_stored * PAIR * POOLED], F32, name="pooled_out"
+                    )
                 nc.vector.scalar_tensor_tensor(
-                    out=pooled_out[b][:, :, pair_of_image * PAIR * POOLED : (pair_of_image + 1) * PAIR * POOLED],
+                    out=pooled_out[first_pair][
+                        :, :, (pair - first_pair) * PAIR * POOLED : (pair - first_pair + 1) * PAIR * POOLED
+                    ],
                     in0=sums[pair][:].rearrange("p (half m) -> p half m", half=HALVES),
                     scalar=1.0 / WINDOW,
                     in1=maxima[pair][:].rearrange("p (half m) -> p half m", half=HALVES),
                     op0=mybir.AluOpType.mult,
                     op1=mybir.AluOpType.add,
                 )
-            if b == IMAGES - 1 and k == PAIR - 1:
-                cols = slice(pair_of_image * PAIR * POOLED, (pair_of_image + 1) * PAIR * POOLED)
-                nc.sync.dma_start(out=pooled_rows[b][:, :, cols], in_=pooled_out[b][:, :, cols])
-            elif c % CHUNKS_PER_IMAGE == CHUNKS_PER_IMAGE - 1:
-                nc.sync.dma_start(out=pooled_rows[b], in_=pooled_out[b][:])
+                if pair == first_pair + pairs_stored - 1:
+                    start = (first_pair % PAIRS_PER_IMAGE) * PAIR * POOLED
+                    nc.sync.dma_start(
+                        out=pooled_rows[b][:, :, start : start + pairs_stored * PAIR * POOLED],
+                        in_=pooled_out[first_pair][:],
+                    )
 
         for step in range(CHUNKS + 2):
             if step < CHUNKS:

@@ -1,6 +1,7 @@
 from contextlib import ExitStack
 
 import concourse.mybir as mybir
+from concourse.masks import make_identity
 
 BF16 = mybir.dt.bfloat16
 F32 = mybir.dt.float32
@@ -25,6 +26,10 @@ WINDOW = 4
 POOLED = CHUNK // WINDOW
 PAIR = 2
 PAIRS_PER_IMAGE = CHUNKS_PER_IMAGE // PAIR
+ROW_PAIRS = CHUNK_ROWS // 2
+PLACE = POOLED * PACK
+LIFTED_PAIRS = 4
+LIFTED = PLACE + LIFTED_PAIRS * (WIDTH // 2) * PACK
 
 FLOPS = 2 * IMAGES * PIXELS * CHANNELS * 2 * OUT_CHANNELS
 
@@ -45,10 +50,14 @@ def tile_selfspatialattentionmodule_pa_t_kernel(
         packed_pool = ctx.enter_context(tc.tile_pool(name="packed", bufs=3))
         conv2_pool = ctx.enter_context(tc.tile_pool(name="conv2", bufs=3))
         pooled_pool = ctx.enter_context(tc.tile_pool(name="pooled", bufs=2))
-        conv1_banks = ctx.enter_context(tc.psum_pool(name="conv1_banks", bufs=3))
-        conv2_banks = ctx.enter_context(tc.psum_pool(name="conv2_banks", bufs=3))
+        conv1_banks = ctx.enter_context(tc.psum_pool(name="conv1_banks", bufs=2))
+        conv2_banks = ctx.enter_context(tc.psum_pool(name="conv2_banks", bufs=2))
         sum_banks = ctx.enter_context(tc.psum_pool(name="sum_banks", bufs=2))
+        lifted_banks = ctx.enter_context(tc.psum_pool(name="lifted_banks", bufs=2))
         ctx.enter_context(tc.manual_schedule())
+
+        identity = keep.tile([P, P], BF16, name="identity")
+        make_identity(nc, identity[:])
 
         raw = {}
         w_words = keep.tile([P, 2, 2 * OUT_CHANNELS], U8, align_bytes=64)
@@ -80,6 +89,7 @@ def tile_selfspatialattentionmodule_pa_t_kernel(
         for b in range(1, IMAGES):
             load_x(b * CHUNKS_PER_IMAGE, CHUNKS_PER_IMAGE)
 
+        lifted = {}
         grouped = {}
         codes = {}
         scales_of = {}
@@ -90,16 +100,25 @@ def tile_selfspatialattentionmodule_pa_t_kernel(
         conv2_out = {}
         pooled_out = {}
 
+        def lift(c):
+            lifted[c] = lifted_banks.tile([P, LIFTED], BF16, name="lifted")
+            by_place = raw[c].rearrange("p t (i dh j dw) -> p dh dw i j t", i=ROW_PAIRS, dh=2, j=WIDTH // 2, dw=2)
+            nc.tensor.matmul(out=lifted[c][:, :PLACE], lhsT=identity[:], rhs=by_place[:, 0, 0], start=True, stop=True)
+            nc.tensor.matmul(
+                out=lifted[c][:, PLACE:], lhsT=identity[:], rhs=by_place[:, 0, 1, :LIFTED_PAIRS], start=True, stop=True
+            )
+
         def regroup(c):
             grouped[c] = grouped_pool.tile([P, PACK * CHUNK], BF16, name="grouped", align_bytes=64)
             nc.scalar.copy(
                 out=grouped[c][:].rearrange(
-                    "p (dh dw i jq jr t) -> p dh i jq t jr dw", dh=2, dw=2, i=CHUNK_ROWS // 2, jq=WIDTH // 4, jr=2, t=PACK
-                )[:, 0],
+                    "p (dh dw i jq jr t) -> p dh dw i jq t jr", dh=2, dw=2, i=ROW_PAIRS, jq=WIDTH // 8, jr=4, t=PACK
+                )[:, 0, 1, LIFTED_PAIRS:],
                 in_=raw[c].rearrange(
-                    "p t (i dh jq jr dw) -> p dh i jq t jr dw", i=CHUNK_ROWS // 2, dh=2, jq=WIDTH // 4, jr=2, dw=2
-                )[:, 0],
+                    "p t (i dh jq jr dw) -> p dh dw i jq t jr", i=ROW_PAIRS, dh=2, jq=WIDTH // 8, jr=4, dw=2
+                )[:, 0, 1, LIFTED_PAIRS:],
             )
+            nc.scalar.copy(out=grouped[c][:, :LIFTED], in_=lifted[c][:])
             nc.gpsimd.tensor_scalar(
                 out=grouped[c][:].rearrange(
                     "p (dh dw i j t) -> p dh i j dw t", dh=2, dw=2, i=CHUNK_ROWS // 2, j=WIDTH // 2, t=PACK
@@ -129,12 +148,6 @@ def tile_selfspatialattentionmodule_pa_t_kernel(
 
         def multiply(c):
             pair, k = divmod(c, PAIR)
-            for half in range(HALVES):
-                conv1[c, half] = conv1_banks.tile([P, CHUNK], F32, name="conv1")
-                multiply_by(0, half, conv1[c, half][:], c, slice(0, CHUNK), True, True)
-            for half in range(HALVES):
-                conv2[c, half] = conv2_banks.tile([P, CHUNK], F32, name="conv2")
-                multiply_by(1, half, conv2[c, half][:], c, slice(0, CHUNK), True, True)
             if k == 0:
                 sums[pair] = sum_banks.tile([P, HALVES * PAIR * POOLED], F32, name="sums")
             for half in range(HALVES):
@@ -149,6 +162,11 @@ def tile_selfspatialattentionmodule_pa_t_kernel(
                         place == 0,
                         place == WINDOW - 1,
                     )
+            for half in range(HALVES):
+                conv1[c, half] = conv1_banks.tile([P, CHUNK], F32, name="conv1")
+                multiply_by(0, half, conv1[c, half][:], c, slice(0, CHUNK), True, True)
+                conv2[c, half] = conv2_banks.tile([P, CHUNK], F32, name="conv2")
+                multiply_by(1, half, conv2[c, half][:], c, slice(0, CHUNK), True, True)
 
         def drain(c):
             b = c // CHUNKS_PER_IMAGE
@@ -203,11 +221,15 @@ def tile_selfspatialattentionmodule_pa_t_kernel(
                         in_=pooled_out[first_pair][:],
                     )
 
+        lift(0)
         for step in range(CHUNKS + 2):
+            if step + 1 < CHUNKS:
+                lift(step + 1)
             if step < CHUNKS:
                 regroup(step)
             if 1 <= step <= CHUNKS:
                 quantise(step - 1)
-                multiply(step - 1)
             if step >= 2:
                 drain(step - 2)
+            if 1 <= step <= CHUNKS:
+                multiply(step - 1)

@@ -28,8 +28,7 @@ PAIR = 2
 PAIRS_PER_IMAGE = CHUNKS_PER_IMAGE // PAIR
 ROW_PAIRS = CHUNK_ROWS // 2
 PLACE = POOLED * PACK
-LIFTED_PAIRS = 4
-LIFTED = PLACE + LIFTED_PAIRS * (WIDTH // 2) * PACK
+LIFTED = PLACE
 
 FLOPS = 2 * IMAGES * PIXELS * CHANNELS * 2 * OUT_CHANNELS
 
@@ -102,10 +101,12 @@ def tile_selfspatialattentionmodule_pa_t_kernel(
 
         def lift(c):
             lifted[c] = lifted_banks.tile([P, LIFTED], BF16, name="lifted")
-            by_place = raw[c].rearrange("p t (i dh j dw) -> p dh dw i j t", i=ROW_PAIRS, dh=2, j=WIDTH // 2, dw=2)
-            nc.tensor.matmul(out=lifted[c][:, :PLACE], lhsT=identity[:], rhs=by_place[:, 0, 0], start=True, stop=True)
             nc.tensor.matmul(
-                out=lifted[c][:, PLACE:], lhsT=identity[:], rhs=by_place[:, 0, 1, :LIFTED_PAIRS], start=True, stop=True
+                out=lifted[c][:].rearrange("p (i j t) -> p t i j", i=ROW_PAIRS, j=WIDTH // 2, t=PACK),
+                lhsT=identity[:],
+                rhs=raw[c].rearrange("p t (i dh j dw) -> p dh dw t i j", i=ROW_PAIRS, dh=2, j=WIDTH // 2, dw=2)[:, 0, 0],
+                start=True,
+                stop=True,
             )
 
         def regroup(c):
@@ -113,10 +114,10 @@ def tile_selfspatialattentionmodule_pa_t_kernel(
             nc.scalar.copy(
                 out=grouped[c][:].rearrange(
                     "p (dh dw i jq jr t) -> p dh dw i jq t jr", dh=2, dw=2, i=ROW_PAIRS, jq=WIDTH // 8, jr=4, t=PACK
-                )[:, 0, 1, LIFTED_PAIRS:],
+                )[:, 0, 1],
                 in_=raw[c].rearrange(
                     "p t (i dh jq jr dw) -> p dh dw i jq t jr", i=ROW_PAIRS, dh=2, jq=WIDTH // 8, jr=4, dw=2
-                )[:, 0, 1, LIFTED_PAIRS:],
+                )[:, 0, 1],
             )
             nc.scalar.copy(out=grouped[c][:, :LIFTED], in_=lifted[c][:])
             nc.gpsimd.tensor_scalar(

@@ -120,11 +120,23 @@ def tile_selfspatialattentionmodule_pa_t_kernel(
                 )[:, 0, 1],
             )
             nc.scalar.copy(out=grouped[c][:, :LIFTED], in_=lifted[c][:])
+            gpsimd_pairs = ROW_PAIRS // 2 if c % PAIR == 0 else ROW_PAIRS
+            if gpsimd_pairs < ROW_PAIRS:
+                nc.vector.tensor_copy(
+                    out=grouped[c][:].rearrange(
+                        "p (dh dw i j t) -> p dh dw i j t", dh=2, dw=2, i=ROW_PAIRS, j=WIDTH // 2, t=PACK
+                    )[:, 1, :, gpsimd_pairs:],
+                    in_=raw[c].rearrange("p t (i dh j dw) -> p dh dw i j t", i=ROW_PAIRS, dh=2, j=WIDTH // 2, dw=2)[
+                        :, 1, :, gpsimd_pairs:
+                    ],
+                )
             nc.gpsimd.tensor_scalar(
                 out=grouped[c][:].rearrange(
-                    "p (dh dw i j t) -> p dh i j dw t", dh=2, dw=2, i=CHUNK_ROWS // 2, j=WIDTH // 2, t=PACK
-                )[:, 1],
-                in0=raw[c].rearrange("p t (i dh j dw) -> p dh i j dw t", i=CHUNK_ROWS // 2, dh=2, j=WIDTH // 2, dw=2)[:, 1],
+                    "p (dh dw i j t) -> p dh i j dw t", dh=2, dw=2, i=ROW_PAIRS, j=WIDTH // 2, t=PACK
+                )[:, 1, :gpsimd_pairs],
+                in0=raw[c].rearrange("p t (i dh j dw) -> p dh i j dw t", i=ROW_PAIRS, dh=2, j=WIDTH // 2, dw=2)[
+                    :, 1, :gpsimd_pairs
+                ],
                 scalar1=1.0,
                 scalar2=0.0,
                 op0=mybir.AluOpType.mult,

@@ -29,6 +29,7 @@ PAIRS_PER_IMAGE = CHUNKS_PER_IMAGE // PAIR
 ROW_PAIRS = CHUNK_ROWS // 2
 PLACE = POOLED * PACK
 LIFTED = PLACE
+VECTOR_PAIRS = 3
 
 FLOPS = 2 * IMAGES * PIXELS * CHANNELS * 2 * OUT_CHANNELS
 
@@ -120,7 +121,7 @@ def tile_selfspatialattentionmodule_pa_t_kernel(
                 )[:, 0, 1],
             )
             nc.scalar.copy(out=grouped[c][:, :LIFTED], in_=lifted[c][:])
-            gpsimd_pairs = ROW_PAIRS // 2 if c % PAIR == 0 else ROW_PAIRS
+            gpsimd_pairs = ROW_PAIRS - VECTOR_PAIRS if c % PAIR == 0 else ROW_PAIRS
             if gpsimd_pairs < ROW_PAIRS:
                 nc.vector.tensor_copy(
                     out=grouped[c][:].rearrange(

from contextlib import ExitStack

import concourse.mybir as mybir
from concourse.masks import make_identity

BF16 = mybir.dt.bfloat16
F32 = mybir.dt.float32
I32 = mybir.dt.int32
U8 = mybir.dt.uint8
U32 = mybir.dt.uint32
FP8X4 = mybir.dt.float8_e4m3fn_x4
FP4X4 = mybir.dt.float4_e2m1fn_x4

P = 128
PACK = 4
IMAGES, CHANNELS, HEIGHT, WIDTH = 4, 512, 64, 32
PIXELS = HEIGHT * WIDTH
OUT_CHANNELS = 256
HALVES = OUT_CHANNELS // P

CHUNK = 512
CHUNK_ROWS = CHUNK // WIDTH
CHUNKS_PER_IMAGE = PIXELS // CHUNK
CHUNKS = IMAGES * CHUNKS_PER_IMAGE
WINDOW = 4
POOLED = CHUNK // WINDOW
PAIR = 2
PAIRS_PER_IMAGE = CHUNKS_PER_IMAGE // PAIR
ROW_PAIRS = CHUNK_ROWS // 2
PLACE = POOLED * PACK
LIFTED = PLACE
VECTOR_PAIRS = 3

FLOPS = 2 * IMAGES * PIXELS * CHANNELS * 2 * OUT_CHANNELS


def tile_selfspatialattentionmodule_pa_t_kernel(
    tc, x, W1_words, W1_scales, W2_words, W2_scales, out_0, out_1
):
    nc = tc.nc
    assert tuple(x.shape) == (IMAGES, CHANNELS, HEIGHT, WIDTH)

    x_rows = x.rearrange("b (p t) r w -> b p t (r w)", t=PACK)
    pooled_rows = out_0.rearrange("b (half p) r w -> b p half (r w)", p=P)
    conv2_rows = out_1.rearrange("b (half p) r w -> b p half (r w)", p=P)

    with ExitStack() as ctx:
        keep = ctx.enter_context(tc.tile_pool(name="keep", bufs=1))
        grouped_pool = ctx.enter_context(tc.tile_pool(name="grouped", bufs=3))
        packed_pool = ctx.enter_context(tc.tile_pool(name="packed", bufs=3))
        conv2_pool = ctx.enter_context(tc.tile_pool(name="conv2", bufs=3))
        pooled_pool = ctx.enter_context(tc.tile_pool(name="pooled", bufs=2))
        conv1_banks = ctx.enter_context(tc.psum_pool(name="conv1_banks", bufs=2))
        conv2_banks = ctx.enter_context(tc.psum_pool(name="conv2_banks", bufs=2))
        sum_banks = ctx.enter_context(tc.psum_pool(name="sum_banks", bufs=2))
        lifted_banks = ctx.enter_context(tc.psum_pool(name="lifted_banks", bufs=2))
        ctx.enter_context(tc.manual_schedule())

        identity = keep.tile([P, P], BF16, name="identity")
        make_identity(nc, identity[:])

        raw = {}
        w_words = keep.tile([P, 2, 2 * OUT_CHANNELS], U8, align_bytes=64)
        w_scales = keep.tile([P, 2, OUT_CHANNELS], U8, align_bytes=64)

        def load_x(first_chunk, chunks):
            b, k = divmod(first_chunk, CHUNKS_PER_IMAGE)
            piece = keep.tile([P, PACK, chunks * CHUNK], BF16, name="raw%d" % first_chunk)
            nc.sync.dma_start(out=piece[:], in_=x_rows[b][:, :, k * CHUNK : (k + chunks) * CHUNK])
            for n in range(chunks):
                raw[first_chunk + n] = piece[:, :, n * CHUNK : (n + 1) * CHUNK]

        def load_weight(w, words, scales):
            nc.sync.dma_start(out=w_words[:, w, :].bitcast(I32), in_=words[0].bitcast(I32))
            for quadrant in range(4):
                nc.sync.dma_start(
                    out=w_scales[32 * quadrant : 32 * (quadrant + 1), w, :].bitcast(I32),
                    in_=scales[0, 4 * quadrant : 4 * (quadrant + 1), :]
                    .bitcast(I32)
                    .unsqueeze(0)
                    .broadcast_to([8, 4, OUT_CHANNELS // 4]),
                )

        load_x(0, 1)
        load_weight(0, W1_words, W1_scales)
        load_x(1, 1)
        load_x(2, 2)
        load_weight(1, W2_words, W2_scales)
        for b in range(1, IMAGES):
            load_x(b * CHUNKS_PER_IMAGE, CHUNKS_PER_IMAGE)

        lifted = {}
        grouped = {}
        codes = {}
        scales_of = {}
        conv1 = {}
        conv2 = {}
        sums = {}
        maxima = {}
        conv2_out = {}
        pooled_out = {}

        def lift(c):
            lifted[c] = lifted_banks.tile([P, LIFTED], BF16, name="lifted")
            nc.tensor.matmul(
                out=lifted[c][:].rearrange("p (i j t) -> p t i j", i=ROW_PAIRS, j=WIDTH // 2, t=PACK),
                lhsT=identity[:],
                rhs=raw[c].rearrange("p t (i dh j dw) -> p dh dw t i j", i=ROW_PAIRS, dh=2, j=WIDTH // 2, dw=2)[:, 0, 0],
                start=True,
                stop=True,
            )

        def regroup(c):
            grouped[c] = grouped_pool.tile([P, PACK * CHUNK], BF16, name="grouped", align_bytes=64)
            nc.scalar.copy(
                out=grouped[c][:].rearrange(
                    "p (dh dw i jq jr t) -> p dh dw i jq t jr", dh=2, dw=2, i=ROW_PAIRS, jq=WIDTH // 8, jr=4, t=PACK
                )[:, 0, 1],
                in_=raw[c].rearrange(
                    "p t (i dh jq jr dw) -> p dh dw i jq t jr", i=ROW_PAIRS, dh=2, jq=WIDTH // 8, jr=4, dw=2
                )[:, 0, 1],
            )
            nc.scalar.copy(out=grouped[c][:, :LIFTED], in_=lifted[c][:])
            gpsimd_pairs = ROW_PAIRS - VECTOR_PAIRS if c % PAIR == 0 else ROW_PAIRS
            if gpsimd_pairs < ROW_PAIRS:
                nc.vector.tensor_copy(
                    out=grouped[c][:].rearrange(
                        "p (dh dw i j t) -> p dh dw i j t", dh=2, dw=2, i=ROW_PAIRS, j=WIDTH // 2, t=PACK
                    )[:, 1, :, gpsimd_pairs:],
                    in_=raw[c].rearrange("p t (i dh j dw) -> p dh dw i j t", i=ROW_PAIRS, dh=2, j=WIDTH // 2, dw=2)[
                        :, 1, :, gpsimd_pairs:
                    ],
                )
            nc.gpsimd.tensor_scalar(
                out=grouped[c][:].rearrange(
                    "p (dh dw i j t) -> p dh i j dw t", dh=2, dw=2, i=ROW_PAIRS, j=WIDTH // 2, t=PACK
                )[:, 1, :gpsimd_pairs],
                in0=raw[c].rearrange("p t (i dh j dw) -> p dh i j dw t", i=ROW_PAIRS, dh=2, j=WIDTH // 2, dw=2)[
                    :, 1, :gpsimd_pairs
                ],
                scalar1=1.0,
                scalar2=0.0,
                op0=mybir.AluOpType.mult,
                op1=mybir.AluOpType.add,
            )

        def quantise(c):
            codes[c] = packed_pool.tile([P, CHUNK], U32, name="codes", align_bytes=64)
            scales_of[c] = packed_pool.tile([P, CHUNK], U8, name="scales", align_bytes=64)
            nc.vector.quantize_mx(out=codes[c][:].bitcast(FP8X4), scales=scales_of[c][:], in_=grouped[c][:])

        def multiply_by(w, half, out, c, cols, start, stop):
            nc.tensor.matmul_mx(
                out=out,
                lhsT=w_words[:, w, half * 2 * P : (half + 1) * 2 * P].bitcast(FP4X4),
                lhsT_scale=w_scales[:, w, half * P : (half + 1) * P],
                rhs=codes[c][:, cols].bitcast(FP8X4),
                rhs_scale=scales_of[c][:, cols],
                start=start,
                stop=stop,
            )

        def multiply(c):
            pair, k = divmod(c, PAIR)
            if k == 0:
                sums[pair] = sum_banks.tile([P, HALVES * PAIR * POOLED], F32, name="sums")
            for half in range(HALVES):
                group = slice((half * PAIR + k) * POOLED, (half * PAIR + k + 1) * POOLED)
                for place in range(WINDOW):
                    multiply_by(
                        0,
                        half,
                        sums[pair][:, group],
                        c,
                        slice(place * POOLED, (place + 1) * POOLED),
                        place == 0,
                        place == WINDOW - 1,
                    )
            for half in range(HALVES):
                conv1[c, half] = conv1_banks.tile([P, CHUNK], F32, name="conv1")
                multiply_by(0, half, conv1[c, half][:], c, slice(0, CHUNK), True, True)
                conv2[c, half] = conv2_banks.tile([P, CHUNK], F32, name="conv2")
                multiply_by(1, half, conv2[c, half][:], c, slice(0, CHUNK), True, True)

        def drain(c):
            b = c // CHUNKS_PER_IMAGE
            pair, k = divmod(c, PAIR)
            chunks_stored = 1 if pair == CHUNKS // PAIR - 1 else PAIR
            pairs_stored = 1 if b == IMAGES - 1 else PAIRS_PER_IMAGE
            first_chunk = c - c % chunks_stored
            first_pair = pair - pair % pairs_stored
            if c == first_chunk:
                conv2_out[first_chunk] = conv2_pool.tile([P, HALVES, chunks_stored * CHUNK], F32, name="conv2_out")
            if k == 0:
                maxima[pair] = pooled_pool.tile([P, HALVES * PAIR * POOLED], F32, name="maxima")
            for half in range(HALVES):
                nc.scalar.copy(
                    out=conv2_out[first_chunk][:, half, (c - first_chunk) * CHUNK : (c - first_chunk + 1) * CHUNK].rearrange(
                        "p (i dh j dw) -> p dh i j dw", i=CHUNK_ROWS // 2, dh=2, j=WIDTH // 2, dw=2
                    ),
                    in_=conv2[c, half][:].rearrange(
                        "p (dh dw i j) -> p dh i j dw", dh=2, dw=2, i=CHUNK_ROWS // 2, j=WIDTH // 2
                    ),
                )
                nc.vector.tensor_reduce(
                    out=maxima[pair][:, (half * PAIR + k) * POOLED : (half * PAIR + k + 1) * POOLED],
                    in_=conv1[c, half][:].rearrange("p (place m) -> p m place", place=WINDOW),
                    axis=mybir.AxisListType.X,
                    op=mybir.AluOpType.max,
                )
            if c == first_chunk + chunks_stored - 1:
                start = (first_chunk % CHUNKS_PER_IMAGE) * CHUNK
                nc.sync.dma_start(
                    out=conv2_rows[b][:, :, start : start + chunks_stored * CHUNK], in_=conv2_out[first_chunk][:]
                )
            if k == PAIR - 1:
                if pair == first_pair:
                    pooled_out[first_pair] = pooled_pool.tile(
                        [P, HALVES, pairs_stored * PAIR * POOLED], F32, name="pooled_out"
                    )
                nc.vector.scalar_tensor_tensor(
                    out=pooled_out[first_pair][
                        :, :, (pair - first_pair) * PAIR * POOLED : (pair - first_pair + 1) * PAIR * POOLED
                    ],
                    in0=sums[pair][:].rearrange("p (half m) -> p half m", half=HALVES),
                    scalar=1.0 / WINDOW,
                    in1=maxima[pair][:].rearrange("p (half m) -> p half m", half=HALVES),
                    op0=mybir.AluOpType.mult,
                    op1=mybir.AluOpType.add,
                )
                if pair == first_pair + pairs_stored - 1:
                    start = (first_pair % PAIRS_PER_IMAGE) * PAIR * POOLED
                    nc.sync.dma_start(
                        out=pooled_rows[b][:, :, start : start + pairs_stored * PAIR * POOLED],
                        in_=pooled_out[first_pair][:],
                    )

        lift(0)
        for step in range(CHUNKS + 2):
            if step + 1 < CHUNKS:
                lift(step + 1)
            if step < CHUNKS:
                regroup(step)
            if 1 <= step <= CHUNKS:
                quantise(step - 1)
            if step >= 2:
                drain(step - 2)
            if 1 <= step <= CHUNKS:
                multiply(step - 1)
